import numpy as np
import ml_dtypes


def mxq(x, axis, fmt="e4m3"):
    dtype, down = {"e4m3": (ml_dtypes.float8_e4m3fn, 7), "e5m2": (ml_dtypes.float8_e5m2, 14)}[fmt]
    v = np.moveaxis(np.asarray(x, np.float32).astype(ml_dtypes.bfloat16).astype(np.float64), axis, -1)
    blocks = v.reshape(v.shape[:-1] + (-1, 32))
    amax = np.abs(blocks).max(-1, keepdims=True)
    byte = np.maximum(np.where(amax > 0, np.frexp(amax)[1] - 1 + 127, 0) - down, 1)
    scale = np.exp2(byte - 127.0)
    codes = (blocks / scale).astype(np.float32).astype(dtype).astype(np.float64)
    return np.moveaxis((codes * scale).reshape(v.shape), -1, axis)


WIDE = False


def mx_kscale(k):
    if not WIDE:
        return np.ones(k)
    levels = np.array([10, -10, 5, -5, 0])
    a = np.random.permutation(np.resize(levels, k // 512 * 4)).reshape(k // 512, 4)
    idx = np.arange(k)
    return np.exp2(a[idx // 512, idx % 128 // 32])


BF16 = ml_dtypes.bfloat16


def bf(x):
    return np.asarray(x, np.float32).astype(BF16)


def f64(x):
    return np.asarray(x).astype(np.float64)


E2M1 = np.array([0.0, 0.5, 1.0, 1.5, 2.0, 3.0, 4.0, 6.0, -0.0, -0.5, -1.0, -1.5, -2.0, -3.0, -4.0, -6.0])


def pack_weight(w, fmt):
    k, n = w.shape
    w = f64(bf(w)).reshape(k // 32, 32, n)
    amax = np.abs(w).max(1)
    if fmt == "e4m3":
        byte = np.frexp(amax)[1] - 1 + 127 - 7
    else:
        mant, ex = np.frexp(amax / 6.0)
        byte = np.where(mant > 0.5, ex, ex - 1) + 127
    byte = np.clip(np.where(amax > 0, byte, 1), 1, 254)
    scaled = (w * np.exp2(127.0 - byte)[:, None, :]).reshape(k, n).astype(np.float32)
    by_word = np.ascontiguousarray(scaled.reshape(k // 512, 128, 4, n).transpose(0, 1, 3, 2))
    if fmt == "e4m3":
        words = by_word.astype(ml_dtypes.float8_e4m3fn).view(np.uint8)
    else:
        c = by_word.astype(ml_dtypes.float4_e2m1fn).view(np.uint8) & 0xF
        words = c[..., 0::2] | (c[..., 1::2] << 4)
    return np.ascontiguousarray(words), np.ascontiguousarray(byte.astype(np.uint8).reshape(k // 512, 16, n))


def unpack_weight(words, scales, fmt):
    g, p, n, _ = words.shape
    if fmt == "e4m3":
        vals = np.ascontiguousarray(words).view(ml_dtypes.float8_e4m3fn).astype(np.float64)
    else:
        nib = np.empty((g, p, n, 4), np.uint8)
        nib[..., 0::2] = words & 0xF
        nib[..., 1::2] = words >> 4
        vals = E2M1[nib]
    vals = vals * np.repeat(np.exp2(scales.astype(np.float64) - 127.0), 8, axis=1)[..., None]
    return vals.transpose(0, 1, 3, 2).reshape(g * 512, n)


B, MI, MO, NL = 128, 1536, 1536, 4
IR_DIMS = tuple(2 * l + 1 for l in range(NL))
FLAT_IN = MI * sum(IR_DIMS)
FMT = "e4m3"


def setup_inputs():
    s = mx_kscale(MI)
    sx = np.concatenate([np.repeat(s, d) for d in IR_DIMS])
    inp = {"x": bf(np.random.standard_normal((B, FLAT_IN)) * sx)}
    for l in range(NL):
        w = np.random.standard_normal((MO, MI)) / np.sqrt(MI) / s[None, :]
        words, scales = pack_weight(w.T, FMT)
        inp["W%d_words" % l] = words
        inp["W%d_scales" % l] = scales
    inp["bias"] = bf(np.random.standard_normal(MO))
    return inp


def reference(x, W0_words, W0_scales, W1_words, W1_scales, W2_words, W2_scales, W3_words, W3_scales, bias):
    x = f64(x)
    outs = []
    start = 0
    packed = ((W0_words, W0_scales), (W1_words, W1_scales), (W2_words, W2_scales), (W3_words, W3_scales))
    for d, (words, scales) in zip(IR_DIMS, packed):
        seg = x[:, start:start + MI * d].reshape(B, MI, d)
        rows = seg.transpose(0, 2, 1).reshape(B * d, MI)
        y = mxq(rows, 1, "e4m3") @ unpack_weight(words, scales, FMT)
        outs.append(y.reshape(B, d, MO).transpose(0, 2, 1).reshape(B, MO * d))
        start += MI * d
    outs[0] = outs[0] + f64(bias)
    return np.concatenate(outs, axis=1)

@@ -1,0 +1,201 @@
+from concourse import mybir
+from concourse.masks import make_identity
+
+F32 = mybir.dt.float32
+BF16 = mybir.dt.bfloat16
+I32 = mybir.dt.int32
+U32 = mybir.dt.uint32
+U8 = mybir.dt.uint8
+FP8X4 = mybir.dt.float8_e4m3fn_x4
+
+P = 128
+CHANNELS = 1536
+K_PASS = 512
+PASSES = CHANNELS // K_PASS
+N_TILE = 512
+N_TILES = CHANNELS // N_TILE
+IR_DIMS = (1, 3, 5, 7)
+SEG_START = (0, 1536, 6144, 13824)
+MAX_DIM = 7
+ORDER = (3, 2, 1, 0)
+STEPS = len(ORDER) * PASSES
+
+FLOPS = 2 * P * sum(IR_DIMS) * CHANNELS * CHANNELS
+
+
+def tile_so3_linear_pa_kernel(
+    tc, x, W0_words, W0_scales, W1_words, W1_scales, W2_words, W2_scales, W3_words, W3_scales, bias, out
+):
+    nc = tc.nc
+    words_in = (W0_words, W1_words, W2_words, W3_words)
+    scales_in = (W0_scales, W1_scales, W2_scales, W3_scales)
+
+    with (
+        tc.tile_pool(name="keep", bufs=1) as keep,
+        tc.tile_pool(name="stage", bufs=2) as stage,
+        tc.psum_pool(name="psum", bufs=4) as psum,
+        tc.manual_schedule(),
+    ):
+        x_raw = {}
+        x_sorted = {}
+        x_grouped = {}
+        x_codes = {}
+        x_scales = {}
+        w_codes = {}
+        w_scales = {}
+        y_banks = {}
+        y_planes = {}
+
+        identity = keep.tile([P, P], F32)
+        make_identity(nc, identity[:])
+        bias_rows = keep.tile([P, CHANNELS], BF16)
+
+        for l in ORDER:
+            planes = keep.tile([P, CHANNELS], U8, name="w_scales%d" % l, align_bytes=64)
+            nc.vector.memset(planes[:].bitcast(I32), 0)
+            w_scales[l] = planes
+
+        def load_x(step):
+            l, g = ORDER[step // PASSES], step % PASSES
+            width = K_PASS * IR_DIMS[l]
+            first = SEG_START[l] + g * width
+            raw = keep.tile([P, width], BF16, name="x_raw", tag="x_raw_%d_%d" % (step // PASSES % 2, g))
+            nc.sync.dma_start(out=raw[:], in_=x[:, first : first + width])
+            x_raw[step] = raw
+
+        def load_w_scales(l):
+            for quadrant in range(4):
+                nc.sync.dma_start(
+                    out=w_scales[l][32 * quadrant : 32 * quadrant + 4 * PASSES, :].bitcast(I32),
+                    in_=scales_in[l][:, 4 * quadrant : 4 * quadrant + 4, :].bitcast(I32),
+                )
+
+        def load_w_codes(l):
+            by_partition = words_in[l].rearrange("g p n t -> p g (n t)")
+            for r in range(N_TILES):
+                codes = keep.tile([P, PASSES, N_TILE], U32, name="w_codes_%d_%d" % (l, r), align_bytes=64)
+                nc.sync.dma_start(
+                    out=codes[:].bitcast(I32),
+                    in_=by_partition[:, :, 4 * N_TILE * r : 4 * N_TILE * (r + 1)].bitcast(I32),
+                )
+                w_codes[(l, r)] = codes
+
+        def sort(step):
+            l = ORDER[step // PASSES]
+            d = IR_DIMS[l]
+            ordered = stage.tile([P, K_PASS * MAX_DIM], BF16, name="x_sorted")
+            nc.vector.tensor_copy(
+                out=ordered[:, : K_PASS * d].rearrange("b (i u p e) -> b i u p e", i=d, u=2, e=2),
+                in_=x_raw[step][:].rearrange("b (p u e i) -> b i u p e", u=2, e=2, i=d),
+            )
+            x_sorted[step] = ordered
+
+        def transpose(step):
+            l = ORDER[step // PASSES]
+            d = IR_DIMS[l]
+            as_words = x_sorted[step][:].bitcast(F32)
+            x_grouped[step] = []
+            for i0 in range(0, d, 2):
+                count = min(2, d - i0)
+                turned = psum.tile([P, 2, 2, P], F32, name="turned")
+                for c in range(count):
+                    for u in range(2):
+                        first = (2 * (i0 + c) + u) * P
+                        nc.tensor.transpose(turned[:, c, u, :], as_words[:, first : first + P], identity[:])
+                grouped = stage.tile([P, 2 * P * 4], BF16, name="grouped", bufs=4, align_bytes=64)
+                nc.scalar.copy(
+                    out=grouped[:].bitcast(F32).rearrange("p (c b u) -> p c b u", c=2, u=2)[:, :count],
+                    in_=turned[:, :count].rearrange("p c u b -> p c b u"),
+                )
+                x_grouped[step].append(grouped)
+
+        def quantise(step):
+            l, g = ORDER[step // PASSES], step % PASSES
+            d = IR_DIMS[l]
+            if g == 0:
+                codes = keep.tile([P, PASSES, d, P], U32, name="x_codes%d" % l, align_bytes=64)
+                scales = keep.tile([P, PASSES, d, P], U8, name="x_scales%d" % l, align_bytes=64)
+                x_codes[l], x_scales[l] = codes, scales
+            for i0 in range(0, d, 2):
+                count = min(2, d - i0)
+                nc.vector.quantize_mx(
+                    out=x_codes[l][:, g, i0 : i0 + count, :].rearrange("p c b -> p (c b)").bitcast(FP8X4),
+                    scales=x_scales[l][:, g, i0 : i0 + count, :].rearrange("p c b -> p (c b)"),
+                    in_=x_grouped[step][i0 // 2][:, : count * P * 4],
+                )
+
+        def multiply(step):
+            l, r = ORDER[step // N_TILES], step % N_TILES
+            d = IR_DIMS[l]
+            if d > 1:
+                planes = stage.tile([P, MAX_DIM, N_TILE], F32, name="y_planes")
+                y_planes[step] = planes
+            for i in range(d):
+                bank = psum.tile([P, N_TILE], F32, name="bank")
+                for g in range(PASSES):
+                    nc.tensor.matmul_mx(
+                        out=bank[:],
+                        lhsT=x_codes[l][:, g, i, :].bitcast(FP8X4),
+                        lhsT_scale=x_scales[l][:, g, i, :],
+                        rhs=w_codes[(l, r)][:, g, :].bitcast(FP8X4),
+                        rhs_scale=w_scales[l][4 * g : P, N_TILE * r : N_TILE * (r + 1)],
+                        start=(g == 0),
+                        stop=(g == PASSES - 1),
+                    )
+                if d > 1:
+                    nc.scalar.copy(out=y_planes[step][:, i, :], in_=bank[:])
+                else:
+                    y_banks[step] = bank
+
+        def finish(step):
+            l, r = ORDER[step // N_TILES], step % N_TILES
+            d = IR_DIMS[l]
+            result = stage.tile([P, N_TILE * MAX_DIM], F32, name="result")
+            if d > 1:
+                nc.vector.tensor_copy(
+                    out=result[:, : N_TILE * d].rearrange("b (n i) -> b n i", i=d),
+                    in_=y_planes[step][:, :d, :].rearrange("b i n -> b n i"),
+                )
+            else:
+                nc.vector.tensor_tensor(
+                    out=result[:, :N_TILE],
+                    in0=y_banks[step][:],
+                    in1=bias_rows[:, N_TILE * r : N_TILE * (r + 1)],
+                    op=mybir.AluOpType.add,
+                )
+            first = SEG_START[l] + N_TILE * d * r
+            nc.sync.dma_start(out=out[:, first : first + N_TILE * d], in_=result[:, : N_TILE * d])
+
+        for step in range(PASSES):
+            load_x(step)
+        for l in ORDER:
+            load_w_scales(l)
+        load_w_codes(ORDER[0])
+        for step in range(PASSES, 2 * PASSES):
+            load_x(step)
+        load_w_codes(ORDER[1])
+
+        sort(0)
+        for step in range(PASSES):
+            sort(step + 1)
+            transpose(step)
+            quantise(step)
+        for step in range(2 * PASSES, 3 * PASSES):
+            load_x(step)
+        load_w_codes(ORDER[2])
+
+        for step in range(STEPS):
+            if step + PASSES + 1 < STEPS:
+                sort(step + PASSES + 1)
+            if step + PASSES + 1 == 2 * PASSES - 1:
+                for late in range(3 * PASSES, STEPS):
+                    load_x(late)
+                nc.sync.dma_start(out=bias_rows[:], in_=bias.partition_broadcast(P))
+                load_w_codes(ORDER[3])
+            if step + PASSES < STEPS:
+                transpose(step + PASSES)
+                quantise(step + PASSES)
+            if step > 0:
+                finish(step - 1)
+            multiply(step)
+        finish(STEPS - 1)

@@ -19,6 +19,8 @@ SEG_START = (0, 1536, 6144, 13824)
 MAX_DIM = 7
 ORDER = (3, 2, 1, 0)
 STEPS = len(ORDER) * PASSES
+OPEN_UNITS = 4
+READ_RUN = 2
 
 FLOPS = 2 * P * sum(IR_DIMS) * CHANNELS * CHANNELS
 
@@ -70,24 +72,28 @@ def tile_so3_linear_pa_kernel(
                     in_=scales_in[l][:, 4 * quadrant : 4 * quadrant + 4, :].bitcast(I32),
                 )
 
-        def load_w_codes(l):
+        def load_w_codes(step):
+            l, r = ORDER[step // N_TILES], step % N_TILES
             by_partition = words_in[l].rearrange("g p n t -> p g (n t)")
-            for r in range(N_TILES):
-                codes = keep.tile([P, PASSES, N_TILE], U32, name="w_codes_%d_%d" % (l, r), align_bytes=64)
-                nc.sync.dma_start(
-                    out=codes[:].bitcast(I32),
-                    in_=by_partition[:, :, 4 * N_TILE * r : 4 * N_TILE * (r + 1)].bitcast(I32),
-                )
-                w_codes[(l, r)] = codes
+            codes = keep.tile([P, PASSES, N_TILE], U32, name="w_codes_%d" % step, align_bytes=64)
+            nc.sync.dma_start(
+                out=codes[:].bitcast(I32),
+                in_=by_partition[:, :, 4 * N_TILE * r : 4 * N_TILE * (r + 1)].bitcast(I32),
+            )
+            w_codes[step] = codes
 
         def sort(step):
             l = ORDER[step // PASSES]
             d = IR_DIMS[l]
             ordered = stage.tile([P, K_PASS * MAX_DIM], BF16, name="x_sorted")
-            nc.vector.tensor_copy(
-                out=ordered[:, : K_PASS * d].rearrange("b (i u p e) -> b i u p e", i=d, u=2, e=2),
-                in_=x_raw[step][:].rearrange("b (p u e i) -> b i u p e", u=2, e=2, i=d),
-            )
+            copies = (d + OPEN_UNITS - 1) // OPEN_UNITS
+            share = (d + copies - 1) // copies
+            for i0 in range(0, d, share):
+                i1 = min(i0 + share, d)
+                nc.vector.tensor_copy(
+                    out=ordered[:, K_PASS * i0 : K_PASS * i1].rearrange("b (i u p e) -> b u p e i", u=2, e=2, p=P),
+                    in_=x_raw[step][:].rearrange("b (p u e i) -> b u p e i", u=2, e=2, i=d)[:, :, :, :, i0:i1],
+                )
             x_sorted[step] = ordered
 
         def transpose(step):
@@ -124,20 +130,20 @@ def tile_so3_linear_pa_kernel(
                     in_=x_grouped[step][i0 // 2][:, : count * P * 4],
                 )
 
-        def multiply(step):
+        def multiply(step, components):
             l, r = ORDER[step // N_TILES], step % N_TILES
             d = IR_DIMS[l]
-            if d > 1:
-                planes = stage.tile([P, MAX_DIM, N_TILE], F32, name="y_planes")
-                y_planes[step] = planes
-            for i in range(d):
+            for i in components:
+                if d > 1 and i == 0:
+                    planes = stage.tile([P, MAX_DIM, N_TILE], F32, name="y_planes")
+                    y_planes[step] = planes
                 bank = psum.tile([P, N_TILE], F32, name="bank")
                 for g in range(PASSES):
                     nc.tensor.matmul_mx(
                         out=bank[:],
                         lhsT=x_codes[l][:, g, i, :].bitcast(FP8X4),
                         lhsT_scale=x_scales[l][:, g, i, :],
-                        rhs=w_codes[(l, r)][:, g, :].bitcast(FP8X4),
+                        rhs=w_codes[step][:, g, :].bitcast(FP8X4),
                         rhs_scale=w_scales[l][4 * g : P, N_TILE * r : N_TILE * (r + 1)],
                         start=(g == 0),
                         stop=(g == PASSES - 1),
@@ -153,8 +159,8 @@ def tile_so3_linear_pa_kernel(
             result = stage.tile([P, N_TILE * MAX_DIM], F32, name="result")
             if d > 1:
                 nc.vector.tensor_copy(
-                    out=result[:, : N_TILE * d].rearrange("b (n i) -> b n i", i=d),
-                    in_=y_planes[step][:, :d, :].rearrange("b i n -> b n i"),
+                    out=result[:, : N_TILE * d].rearrange("b (m n i) -> b m i n", n=READ_RUN, i=d),
+                    in_=y_planes[step][:, :d, :].rearrange("b i (m n) -> b m i n", n=READ_RUN),
                 )
             else:
                 nc.vector.tensor_tensor(
@@ -170,32 +176,37 @@ def tile_so3_linear_pa_kernel(
             load_x(step)
         for l in ORDER:
             load_w_scales(l)
-        load_w_codes(ORDER[0])
+        for step in range(PASSES):
+            load_w_codes(step)
+            load_x(step + PASSES)
         for step in range(PASSES, 2 * PASSES):
-            load_x(step)
-        load_w_codes(ORDER[1])
+            load_w_codes(step)
 
         sort(0)
-        for step in range(PASSES):
-            sort(step + 1)
-            transpose(step)
-            quantise(step)
-        for step in range(2 * PASSES, 3 * PASSES):
-            load_x(step)
-        load_w_codes(ORDER[2])
+        sort(1)
+        transpose(0)
+        quantise(0)
+        sort(2)
+        transpose(1)
+        quantise(1)
+        transpose(2)
+        quantise(2)
+        sort(3)
 
         for step in range(STEPS):
+            d = IR_DIMS[ORDER[step // N_TILES]]
+            multiply(step, range(d // 2))
+            if step > 0:
+                finish(step - 1)
+            if step + 2 * PASSES < STEPS:
+                load_x(step + 2 * PASSES)
+                load_w_codes(step + 2 * PASSES)
+            if step + 2 * PASSES == STEPS - 1:
+                nc.sync.dma_start(out=bias_rows[:], in_=bias.partition_broadcast(P))
             if step + PASSES + 1 < STEPS:
                 sort(step + PASSES + 1)
-            if step + PASSES + 1 == 2 * PASSES - 1:
-                for late in range(3 * PASSES, STEPS):
-                    load_x(late)
-                nc.sync.dma_start(out=bias_rows[:], in_=bias.partition_broadcast(P))
-                load_w_codes(ORDER[3])
             if step + PASSES < STEPS:
                 transpose(step + PASSES)
                 quantise(step + PASSES)
-            if step > 0:
-                finish(step - 1)
-            multiply(step)
+            multiply(step, range(d // 2, d))
         finish(STEPS - 1)

@@ -50,6 +50,11 @@ def tile_so3_linear_pa_kernel(
 
         identity = keep.tile([P, P], F32)
         make_identity(nc, identity[:])
+        bias_row = keep.tile([P, CHANNELS], BF16)
+        nc.vector.memset(bias_row[:], 0.0)
+        nc.scalar.dma_start(out=bias_row[0:1, :], in_=bias.unsqueeze(0))
+        ones = keep.tile([P, P], BF16)
+        nc.vector.memset(ones[:], 1.0)
         bias_rows = keep.tile([P, CHANNELS], BF16)
 
         for l in ORDER:
@@ -67,20 +72,26 @@ def tile_so3_linear_pa_kernel(
 
         def load_w_scales(l):
             for quadrant in range(4):
-                nc.sync.dma_start(
-                    out=w_scales[l][32 * quadrant : 32 * quadrant + 4 * PASSES, :].bitcast(I32),
-                    in_=scales_in[l][:, 4 * quadrant : 4 * quadrant + 4, :].bitcast(I32),
+                nc.gpsimd.dma_start(
+                    out=w_scales[l][32 * quadrant : 32 * quadrant + 4 * PASSES, :].bitcast(F32),
+                    in_=scales_in[l][:, 4 * quadrant : 4 * quadrant + 4, :].bitcast(F32),
                 )
 
         def load_w_codes(step):
-            l, r = ORDER[step // N_TILES], step % N_TILES
-            by_partition = words_in[l].rearrange("g p n t -> p g (n t)")
-            codes = keep.tile([P, PASSES, N_TILE], U32, name="w_codes_%d" % step, align_bytes=64)
+            l, g = ORDER[step // PASSES], step % PASSES
+            codes = keep.tile([P, CHANNELS], U32, name="w_codes_%d" % step, align_bytes=64)
             nc.sync.dma_start(
                 out=codes[:].bitcast(I32),
-                in_=by_partition[:, :, 4 * N_TILE * r : 4 * N_TILE * (r + 1)].bitcast(I32),
+                in_=words_in[l][g].rearrange("p n t -> p (n t)").bitcast(I32),
             )
             w_codes[step] = codes
+
+        def spread_bias():
+            for r in range(N_TILES):
+                n_cols = slice(N_TILE * r, N_TILE * (r + 1))
+                bank = psum.tile([P, N_TILE], F32, name="bank")
+                nc.tensor.matmul(out=bank[:], lhsT=ones[:], rhs=bias_row[:, n_cols], start=True, stop=True)
+                nc.scalar.copy(out=bias_rows[:, n_cols], in_=bank[:])
 
         def sort(step):
             l = ORDER[step // PASSES]
@@ -143,7 +154,7 @@ def tile_so3_linear_pa_kernel(
                         out=bank[:],
                         lhsT=x_codes[l][:, g, i, :].bitcast(FP8X4),
                         lhsT_scale=x_scales[l][:, g, i, :],
-                        rhs=w_codes[step][:, g, :].bitcast(FP8X4),
+                        rhs=w_codes[step - r + g][:, N_TILE * r : N_TILE * (r + 1)].bitcast(FP8X4),
                         rhs_scale=w_scales[l][4 * g : P, N_TILE * r : N_TILE * (r + 1)],
                         start=(g == 0),
                         stop=(g == PASSES - 1),
@@ -172,15 +183,15 @@ def tile_so3_linear_pa_kernel(
             first = SEG_START[l] + N_TILE * d * r
             nc.sync.dma_start(out=out[:, first : first + N_TILE * d], in_=result[:, : N_TILE * d])
 
-        for step in range(PASSES):
-            load_x(step)
         for l in ORDER:
             load_w_scales(l)
-        for step in range(PASSES):
-            load_w_codes(step)
-            load_x(step + PASSES)
-        for step in range(PASSES, 2 * PASSES):
-            load_w_codes(step)
+        for first in (0, PASSES):
+            for step in range(first, first + PASSES):
+                load_x(step)
+            for step in range(first, first + PASSES):
+                load_w_codes(step)
+
+        spread_bias()
 
         sort(0)
         sort(1)
@@ -196,13 +207,11 @@ def tile_so3_linear_pa_kernel(
         for step in range(STEPS):
             d = IR_DIMS[ORDER[step // N_TILES]]
             multiply(step, range(d // 2))
-            if step > 0:
-                finish(step - 1)
             if step + 2 * PASSES < STEPS:
                 load_x(step + 2 * PASSES)
                 load_w_codes(step + 2 * PASSES)
-            if step + 2 * PASSES == STEPS - 1:
-                nc.sync.dma_start(out=bias_rows[:], in_=bias.partition_broadcast(P))
+            if step > 0:
+                finish(step - 1)
             if step + PASSES + 1 < STEPS:
                 sort(step + PASSES + 1)
             if step + PASSES < STEPS:

@@ -50,7 +50,7 @@ def tile_so3_linear_pa_kernel(
 
         identity = keep.tile([P, P], F32)
         make_identity(nc, identity[:])
-        bias_row = keep.tile([P, CHANNELS], BF16)
+        bias_row = stage.tile([P, CHANNELS], BF16, name="bias_row", tag="y_planes")
         nc.vector.memset(bias_row[:], 0.0)
         nc.scalar.dma_start(out=bias_row[0:1, :], in_=bias.unsqueeze(0))
         ones = keep.tile([P, P], BF16)
@@ -167,13 +167,14 @@ def tile_so3_linear_pa_kernel(
         def finish(step):
             l, r = ORDER[step // N_TILES], step % N_TILES
             d = IR_DIMS[l]
-            result = stage.tile([P, N_TILE * MAX_DIM], F32, name="result")
             if d > 1:
+                result = stage.tile([P, N_TILE * MAX_DIM], F32, name="result")
                 nc.vector.tensor_copy(
                     out=result[:, : N_TILE * d].rearrange("b (m n i) -> b m i n", n=READ_RUN, i=d),
                     in_=y_planes[step][:, :d, :].rearrange("b i (m n) -> b m i n", n=READ_RUN),
                 )
             else:
+                result = stage.tile([P, N_TILE], F32, name="result_one", bufs=N_TILES)
                 nc.vector.tensor_tensor(
                     out=result[:, :N_TILE],
                     in0=y_banks[step][:],

@@ -17,7 +17,8 @@ N_TILES = CHANNELS // N_TILE
 IR_DIMS = (1, 3, 5, 7)
 SEG_START = (0, 1536, 6144, 13824)
 MAX_DIM = 7
-ORDER = (3, 2, 1, 0)
+ORDER = (1, 3, 2, 0)
+SMALL_DIM = 3
 STEPS = len(ORDER) * PASSES
 OPEN_UNITS = 4
 READ_RUN = 2
@@ -47,54 +48,60 @@ def tile_so3_linear_pa_kernel(
         w_scales = {}
         y_banks = {}
         y_planes = {}
+        results = {}
 
+        bias_in = keep.tile([1, CHANNELS], BF16)
+        nc.scalar.dma_start(out=bias_in[:], in_=bias.unsqueeze(0))
         identity = keep.tile([P, P], F32)
         make_identity(nc, identity[:])
         bias_row = stage.tile([P, CHANNELS], BF16, name="bias_row", tag="y_planes")
-        nc.vector.memset(bias_row[:], 0.0)
-        nc.scalar.dma_start(out=bias_row[0:1, :], in_=bias.unsqueeze(0))
         ones = keep.tile([P, P], BF16)
-        nc.vector.memset(ones[:], 1.0)
         bias_rows = keep.tile([P, CHANNELS], BF16)
 
         for l in ORDER:
             planes = keep.tile([P, CHANNELS], U8, name="w_scales%d" % l, align_bytes=64)
             nc.vector.memset(planes[:].bitcast(I32), 0)
             w_scales[l] = planes
+            if l == ORDER[0]:
+                nc.vector.memset(bias_row[:], 0.0)
+                nc.vector.memset(ones[:], 1.0)
 
-        def load_x(step):
-            l, g = ORDER[step // PASSES], step % PASSES
+        def load_x(chunk):
+            l, g = ORDER[chunk // PASSES], chunk % PASSES
             width = K_PASS * IR_DIMS[l]
             first = SEG_START[l] + g * width
-            raw = keep.tile([P, width], BF16, name="x_raw", tag="x_raw_%d_%d" % (step // PASSES % 2, g))
+            raw = keep.tile([P, width], BF16, name="x_raw", tag="x_raw_%d_%d" % (chunk // PASSES % 2, g))
             nc.sync.dma_start(out=raw[:], in_=x[:, first : first + width])
-            x_raw[step] = raw
+            x_raw[chunk] = raw
 
-        def load_w_scales(l):
+        def load_w_scales(l, queue):
             for quadrant in range(4):
-                nc.gpsimd.dma_start(
+                queue.dma_start(
                     out=w_scales[l][32 * quadrant : 32 * quadrant + 4 * PASSES, :].bitcast(F32),
                     in_=scales_in[l][:, 4 * quadrant : 4 * quadrant + 4, :].bitcast(F32),
                 )
 
         def load_w_codes(step):
-            l, g = ORDER[step // PASSES], step % PASSES
-            codes = keep.tile([P, CHANNELS], U32, name="w_codes_%d" % step, align_bytes=64)
+            l, r = ORDER[step // N_TILES], step % N_TILES
+            codes = keep.tile(
+                [P, PASSES, N_TILE], U32, name="w_codes", tag="w_codes_%d_%d" % (step // N_TILES % 3, r), align_bytes=64
+            )
             nc.sync.dma_start(
                 out=codes[:].bitcast(I32),
-                in_=words_in[l][g].rearrange("p n t -> p (n t)").bitcast(I32),
+                in_=words_in[l].rearrange("g p n t -> p g (n t)")[:, :, 4 * N_TILE * r : 4 * N_TILE * (r + 1)].bitcast(I32),
             )
             w_codes[step] = codes
 
         def spread_bias():
+            nc.vector.tensor_copy(out=bias_row[0:1, :], in_=bias_in[:])
             for r in range(N_TILES):
                 n_cols = slice(N_TILE * r, N_TILE * (r + 1))
                 bank = psum.tile([P, N_TILE], F32, name="bank")
                 nc.tensor.matmul(out=bank[:], lhsT=ones[:], rhs=bias_row[:, n_cols], start=True, stop=True)
                 nc.scalar.copy(out=bias_rows[:, n_cols], in_=bank[:])
 
-        def sort(step):
-            l = ORDER[step // PASSES]
+        def sort(chunk):
+            l = ORDER[chunk // PASSES]
             d = IR_DIMS[l]
             ordered = stage.tile([P, K_PASS * MAX_DIM], BF16, name="x_sorted")
             copies = (d + OPEN_UNITS - 1) // OPEN_UNITS
@@ -103,15 +110,15 @@ def tile_so3_linear_pa_kernel(
                 i1 = min(i0 + share, d)
                 nc.vector.tensor_copy(
                     out=ordered[:, K_PASS * i0 : K_PASS * i1].rearrange("b (i u p e) -> b u p e i", u=2, e=2, p=P),
-                    in_=x_raw[step][:].rearrange("b (p u e i) -> b u p e i", u=2, e=2, i=d)[:, :, :, :, i0:i1],
+                    in_=x_raw[chunk][:].rearrange("b (p u e i) -> b u p e i", u=2, e=2, i=d)[:, :, :, :, i0:i1],
                 )
-            x_sorted[step] = ordered
+            x_sorted[chunk] = ordered
 
-        def transpose(step):
-            l = ORDER[step // PASSES]
+        def transpose(chunk):
+            l = ORDER[chunk // PASSES]
             d = IR_DIMS[l]
-            as_words = x_sorted[step][:].bitcast(F32)
-            x_grouped[step] = []
+            as_words = x_sorted[chunk][:].bitcast(F32)
+            x_grouped[chunk] = []
             for i0 in range(0, d, 2):
                 count = min(2, d - i0)
                 turned = psum.tile([P, 2, 2, P], F32, name="turned")
@@ -124,10 +131,10 @@ def tile_so3_linear_pa_kernel(
                     out=grouped[:].bitcast(F32).rearrange("p (c b u) -> p c b u", c=2, u=2)[:, :count],
                     in_=turned[:, :count].rearrange("p c u b -> p c b u"),
                 )
-                x_grouped[step].append(grouped)
+                x_grouped[chunk].append(grouped)
 
-        def quantise(step):
-            l, g = ORDER[step // PASSES], step % PASSES
+        def quantise(chunk):
+            l, g = ORDER[chunk // PASSES], chunk % PASSES
             d = IR_DIMS[l]
             if g == 0:
                 codes = keep.tile([P, PASSES, d, P], U32, name="x_codes%d" % l, align_bytes=64)
@@ -138,85 +145,123 @@ def tile_so3_linear_pa_kernel(
                 nc.vector.quantize_mx(
                     out=x_codes[l][:, g, i0 : i0 + count, :].rearrange("p c b -> p (c b)").bitcast(FP8X4),
                     scales=x_scales[l][:, g, i0 : i0 + count, :].rearrange("p c b -> p (c b)"),
-                    in_=x_grouped[step][i0 // 2][:, : count * P * 4],
+                    in_=x_grouped[chunk][i0 // 2][:, : count * P * 4],
                 )
 
-        def multiply(step, components):
+        def passes(step, i, some_passes):
             l, r = ORDER[step // N_TILES], step % N_TILES
             d = IR_DIMS[l]
-            for i in components:
-                if d > 1 and i == 0:
-                    planes = stage.tile([P, MAX_DIM, N_TILE], F32, name="y_planes")
-                    y_planes[step] = planes
-                bank = psum.tile([P, N_TILE], F32, name="bank")
-                for g in range(PASSES):
-                    nc.tensor.matmul_mx(
-                        out=bank[:],
-                        lhsT=x_codes[l][:, g, i, :].bitcast(FP8X4),
-                        lhsT_scale=x_scales[l][:, g, i, :],
-                        rhs=w_codes[step - r + g][:, N_TILE * r : N_TILE * (r + 1)].bitcast(FP8X4),
-                        rhs_scale=w_scales[l][4 * g : P, N_TILE * r : N_TILE * (r + 1)],
-                        start=(g == 0),
-                        stop=(g == PASSES - 1),
-                    )
-                if d > 1:
-                    nc.scalar.copy(out=y_planes[step][:, i, :], in_=bank[:])
-                else:
-                    y_banks[step] = bank
+            for g in some_passes:
+                if g == 0:
+                    if d > 1 and i == 0:
+                        planes = stage.tile([P, MAX_DIM, N_TILE], F32, name="y_planes")
+                        y_planes[step] = planes
+                    bank = psum.tile([P, N_TILE], F32, name="bank")
+                    y_banks[(step, i)] = bank
+                nc.tensor.matmul_mx(
+                    out=y_banks[(step, i)][:],
+                    lhsT=x_codes[l][:, g, i, :].bitcast(FP8X4),
+                    lhsT_scale=x_scales[l][:, g, i, :],
+                    rhs=w_codes[step][:, g, :].bitcast(FP8X4),
+                    rhs_scale=w_scales[l][4 * g : P, N_TILE * r : N_TILE * (r + 1)],
+                    start=(g == 0),
+                    stop=(g == PASSES - 1),
+                )
+                if g == PASSES - 1 and d > 1:
+                    nc.scalar.copy(out=y_planes[step][:, i, :], in_=y_banks[(step, i)][:])
 
-        def finish(step):
+        def multiply(step, components):
+            for i in components:
+                passes(step, i, range(PASSES))
+
+        def interleave(step):
             l, r = ORDER[step // N_TILES], step % N_TILES
             d = IR_DIMS[l]
-            if d > 1:
+            if d > SMALL_DIM:
                 result = stage.tile([P, N_TILE * MAX_DIM], F32, name="result")
+            else:
+                result = stage.tile([P, N_TILE * SMALL_DIM], F32, name="result_small", bufs=N_TILES)
+            if d > 1:
                 nc.vector.tensor_copy(
                     out=result[:, : N_TILE * d].rearrange("b (m n i) -> b m i n", n=READ_RUN, i=d),
                     in_=y_planes[step][:, :d, :].rearrange("b i (m n) -> b m i n", n=READ_RUN),
                 )
             else:
-                result = stage.tile([P, N_TILE], F32, name="result_one", bufs=N_TILES)
                 nc.vector.tensor_tensor(
                     out=result[:, :N_TILE],
-                    in0=y_banks[step][:],
+                    in0=y_banks[(step, 0)][:],
                     in1=bias_rows[:, N_TILE * r : N_TILE * (r + 1)],
                     op=mybir.AluOpType.add,
                 )
-            first = SEG_START[l] + N_TILE * d * r
-            nc.sync.dma_start(out=out[:, first : first + N_TILE * d], in_=result[:, : N_TILE * d])
+            results[step] = result
 
-        for l in ORDER:
-            load_w_scales(l)
-        for first in (0, PASSES):
-            for step in range(first, first + PASSES):
-                load_x(step)
-            for step in range(first, first + PASSES):
-                load_w_codes(step)
+        def store(step):
+            l, r = ORDER[step // N_TILES], step % N_TILES
+            d = IR_DIMS[l]
+            first = SEG_START[l] + N_TILE * d * r
+            nc.sync.dma_start(out=out[:, first : first + N_TILE * d], in_=results[step][:, : N_TILE * d])
+
+        load_w_scales(ORDER[0], nc.scalar)
+        for l in ORDER[1:]:
+            load_w_scales(l, nc.gpsimd)
+        for chunk in range(PASSES):
+            load_x(chunk)
+        for r in range(N_TILES):
+            load_w_codes(r)
+            load_x(PASSES + r)
+        for r in range(N_TILES):
+            load_w_codes(N_TILES + r)
 
         spread_bias()
-
         sort(0)
         sort(1)
         transpose(0)
         quantise(0)
         sort(2)
+        for chunk in range(2 * PASSES, 3 * PASSES):
+            load_x(chunk)
         transpose(1)
         quantise(1)
         transpose(2)
         quantise(2)
         sort(3)
 
-        for step in range(STEPS):
+        for step in range(N_TILES):
+            multiply(step, range(IR_DIMS[ORDER[0]]))
+            transpose(step + PASSES)
+            if step < N_TILES - 1:
+                interleave(step)
+                store(step)
+                sort(step + PASSES + 1)
+                quantise(step + PASSES)
+            else:
+                quantise(step + PASSES)
+                interleave(step)
+                store(step)
+                sort(step + PASSES + 1)
+
+        for step in range(N_TILES, STEPS):
             d = IR_DIMS[ORDER[step // N_TILES]]
-            multiply(step, range(d // 2))
+            front = range((d + 1) // 2)
+            if step == N_TILES:
+                for g in range(PASSES):
+                    for i in front:
+                        passes(step, i, (g,))
+            else:
+                multiply(step, front)
             if step + 2 * PASSES < STEPS:
+                load_w_codes(step + N_TILES)
                 load_x(step + 2 * PASSES)
-                load_w_codes(step + 2 * PASSES)
-            if step > 0:
-                finish(step - 1)
+            elif step + PASSES < STEPS:
+                load_w_codes(step + N_TILES)
+            if step > N_TILES:
+                interleave(step - 1)
+                store(step - 1)
             if step + PASSES + 1 < STEPS:
                 sort(step + PASSES + 1)
             if step + PASSES < STEPS:
                 transpose(step + PASSES)
                 quantise(step + PASSES)
-            multiply(step, range(d // 2, d))
-        finish(STEPS - 1)
+            multiply(step, range((d + 1) // 2, d))
+        interleave(STEPS - 1)
+        store(STEPS - 1)

@@ -18,6 +18,7 @@ IR_DIMS = (1, 3, 5, 7)
 SEG_START = (0, 1536, 6144, 13824)
 MAX_DIM = 7
 ORDER = (1, 3, 2, 0)
+PIECES = {8: 4, 7: 2}
 SMALL_DIM = 3
 STEPS = len(ORDER) * PASSES
 OPEN_UNITS = 4
@@ -60,7 +61,10 @@ def tile_so3_linear_pa_kernel(
 
         for l in ORDER:
             planes = keep.tile([P, CHANNELS], U8, name="w_scales%d" % l, align_bytes=64)
-            nc.vector.memset(planes[:].bitcast(I32), 0)
+            if l in ORDER[:2]:
+                nc.vector.memset(planes[:].bitcast(I32), 0)
+            else:
+                nc.gpsimd.memset(planes[:].bitcast(F32), 0.0)
             w_scales[l] = planes
             if l == ORDER[0]:
                 nc.vector.memset(bias_row[:], 0.0)
@@ -94,16 +98,23 @@ def tile_so3_linear_pa_kernel(
 
         def spread_bias():
             nc.vector.tensor_copy(out=bias_row[0:1, :], in_=bias_in[:])
-            for r in range(N_TILES):
-                n_cols = slice(N_TILE * r, N_TILE * (r + 1))
-                bank = psum.tile([P, N_TILE], F32, name="bank")
-                nc.tensor.matmul(out=bank[:], lhsT=ones[:], rhs=bias_row[:, n_cols], start=True, stop=True)
-                nc.scalar.copy(out=bias_rows[:, n_cols], in_=bank[:])
+            for first in range(0, CHANNELS, 2 * N_TILE):
+                width = min(2 * N_TILE, CHANNELS - first)
+                bank = psum.tile([P, 2 * N_TILE], BF16, name="bank")
+                for n0 in range(0, width, N_TILE):
+                    nc.tensor.matmul(
+                        out=bank[:, n0 : n0 + N_TILE], lhsT=ones[:], rhs=bias_row[:, first + n0 : first + n0 + N_TILE],
+                        start=True, stop=True,
+                    )
+                nc.scalar.copy(out=bias_rows[:, first : first + width], in_=bank[:, :width])
 
         def sort(chunk):
             l = ORDER[chunk // PASSES]
             d = IR_DIMS[l]
-            ordered = stage.tile([P, K_PASS * MAX_DIM], BF16, name="x_sorted")
+            if chunk < PASSES:
+                ordered = stage.tile([P, K_PASS * SMALL_DIM], BF16, name="x_sorted_first", bufs=PASSES)
+            else:
+                ordered = stage.tile([P, K_PASS * MAX_DIM], BF16, name="x_sorted")
             copies = (d + OPEN_UNITS - 1) // OPEN_UNITS
             share = (d + copies - 1) // copies
             for i0 in range(0, d, share):
@@ -182,10 +193,19 @@ def tile_so3_linear_pa_kernel(
             else:
                 result = stage.tile([P, N_TILE * SMALL_DIM], F32, name="result_small", bufs=N_TILES)
             if d > 1:
-                nc.vector.tensor_copy(
-                    out=result[:, : N_TILE * d].rearrange("b (m n i) -> b m i n", n=READ_RUN, i=d),
-                    in_=y_planes[step][:, :d, :].rearrange("b i (m n) -> b m i n", n=READ_RUN),
-                )
+                pieces = PIECES.get(step, 1)
+                width = N_TILE // pieces
+                first = SEG_START[l] + N_TILE * d * r
+                for k in range(pieces):
+                    nc.vector.tensor_copy(
+                        out=result[:, width * d * k : width * d * (k + 1)].rearrange("b (m n i) -> b m i n", n=READ_RUN, i=d),
+                        in_=y_planes[step][:, :d, width * k : width * (k + 1)].rearrange("b i (m n) -> b m i n", n=READ_RUN),
+                    )
+                    if pieces > 1:
+                        nc.sync.dma_start(
+                            out=out[:, first + width * d * k : first + width * d * (k + 1)],
+                            in_=result[:, width * d * k : width * d * (k + 1)],
+                        )
             else:
                 nc.vector.tensor_tensor(
                     out=result[:, :N_TILE],
@@ -198,6 +218,8 @@ def tile_so3_linear_pa_kernel(
         def store(step):
             l, r = ORDER[step // N_TILES], step % N_TILES
             d = IR_DIMS[l]
+            if PIECES.get(step, 1) > 1:
+                return
             first = SEG_START[l] + N_TILE * d * r
             nc.sync.dma_start(out=out[:, first : first + N_TILE * d], in_=results[step][:, : N_TILE * d])
 
@@ -215,11 +237,11 @@ def tile_so3_linear_pa_kernel(
         spread_bias()
         sort(0)
         sort(1)
-        transpose(0)
-        quantise(0)
         sort(2)
         for chunk in range(2 * PASSES, 3 * PASSES):
             load_x(chunk)
+        transpose(0)
+        quantise(0)
         transpose(1)
         quantise(1)
         transpose(2)
@@ -249,14 +271,19 @@ def tile_so3_linear_pa_kernel(
                         passes(step, i, (g,))
             else:
                 multiply(step, front)
-            if step + 2 * PASSES < STEPS:
-                load_w_codes(step + N_TILES)
-                load_x(step + 2 * PASSES)
-            elif step + PASSES < STEPS:
-                load_w_codes(step + N_TILES)
+            if step == N_TILES:
+                for later in range(2 * N_TILES, 3 * N_TILES):
+                    load_w_codes(later)
             if step > N_TILES:
                 interleave(step - 1)
                 store(step - 1)
+            if step == N_TILES + 1:
+                for later in range(3 * N_TILES, STEPS):
+                    load_x(later)
+                load_w_codes(3 * N_TILES)
+            if step == N_TILES + 2:
+                load_w_codes(3 * N_TILES + 1)
+                load_w_codes(3 * N_TILES + 2)
             if step + PASSES + 1 < STEPS:
                 sort(step + PASSES + 1)
             if step + PASSES < STEPS:

@@ -18,6 +18,7 @@ IR_DIMS = (1, 3, 5, 7)
 SEG_START = (0, 1536, 6144, 13824)
 MAX_DIM = 7
 ORDER = (1, 3, 2, 0)
+LAST_CHUNK = 9
 PIECES = {8: 4, 7: 2}
 SMALL_DIM = 3
 STEPS = len(ORDER) * PASSES
@@ -70,13 +71,13 @@ def tile_so3_linear_pa_kernel(
                 nc.vector.memset(bias_row[:], 0.0)
                 nc.vector.memset(ones[:], 1.0)
 
-        def load_x(chunk):
-            l, g = ORDER[chunk // PASSES], chunk % PASSES
+        def load_x(l, some_passes):
+            if l not in x_raw:
+                raw = keep.tile([P, CHANNELS * IR_DIMS[l]], BF16, name="x_raw", tag="x_raw_%d" % (ORDER.index(l) % 2))
+                x_raw[l] = raw
             width = K_PASS * IR_DIMS[l]
-            first = SEG_START[l] + g * width
-            raw = keep.tile([P, width], BF16, name="x_raw", tag="x_raw_%d_%d" % (chunk // PASSES % 2, g))
-            nc.sync.dma_start(out=raw[:], in_=x[:, first : first + width])
-            x_raw[chunk] = raw
+            a, b = width * some_passes[0], width * (some_passes[-1] + 1)
+            nc.sync.dma_start(out=x_raw[l][:, a:b], in_=x[:, SEG_START[l] + a : SEG_START[l] + b])
 
         def load_w_scales(l, queue):
             for quadrant in range(4):
@@ -85,16 +86,15 @@ def tile_so3_linear_pa_kernel(
                     in_=scales_in[l][:, 4 * quadrant : 4 * quadrant + 4, :].bitcast(F32),
                 )
 
-        def load_w_codes(step):
-            l, r = ORDER[step // N_TILES], step % N_TILES
-            codes = keep.tile(
-                [P, PASSES, N_TILE], U32, name="w_codes", tag="w_codes_%d_%d" % (step // N_TILES % 3, r), align_bytes=64
-            )
+        def load_w_codes(l, tiles, place):
+            a, b = N_TILE * tiles[0], N_TILE * (tiles[-1] + 1)
+            codes = keep.tile([P, PASSES, b - a], U32, name="w_codes", tag="w_codes_%d_%d" % (place, tiles[0]), align_bytes=64)
             nc.sync.dma_start(
                 out=codes[:].bitcast(I32),
-                in_=words_in[l].rearrange("g p n t -> p g (n t)")[:, :, 4 * N_TILE * r : 4 * N_TILE * (r + 1)].bitcast(I32),
+                in_=words_in[l].rearrange("g p n t -> p g (n t)")[:, :, 4 * a : 4 * b].bitcast(I32),
             )
-            w_codes[step] = codes
+            for r in tiles:
+                w_codes[(l, r)] = codes[:, :, N_TILE * r - a : N_TILE * (r + 1) - a]
 
         def spread_bias():
             nc.vector.tensor_copy(out=bias_row[0:1, :], in_=bias_in[:])
@@ -109,8 +109,16 @@ def tile_so3_linear_pa_kernel(
                 nc.scalar.copy(out=bias_rows[:, first : first + width], in_=bank[:, :width])
 
         def sort(chunk):
-            l = ORDER[chunk // PASSES]
+            l, g = ORDER[chunk // PASSES], chunk % PASSES
             d = IR_DIMS[l]
+            if d == 1:
+                ordered = stage.tile([P, K_PASS * MAX_DIM], BF16, name="x_sorted")
+                nc.vector.tensor_copy(
+                    out=ordered[:, :CHANNELS].rearrange("b (g u p e) -> b g u p e", u=2, e=2, p=P),
+                    in_=x_raw[l][:].rearrange("b (g p u e) -> b g u p e", u=2, e=2, p=P),
+                )
+                x_sorted[chunk] = ordered
+                return
             if chunk < PASSES:
                 ordered = stage.tile([P, K_PASS * SMALL_DIM], BF16, name="x_sorted_first", bufs=PASSES)
             else:
@@ -121,13 +129,15 @@ def tile_so3_linear_pa_kernel(
                 i1 = min(i0 + share, d)
                 nc.vector.tensor_copy(
                     out=ordered[:, K_PASS * i0 : K_PASS * i1].rearrange("b (i u p e) -> b u p e i", u=2, e=2, p=P),
-                    in_=x_raw[chunk][:].rearrange("b (p u e i) -> b u p e i", u=2, e=2, i=d)[:, :, :, :, i0:i1],
+                    in_=x_raw[l][:, K_PASS * d * g : K_PASS * d * (g + 1)].rearrange("b (p u e i) -> b u p e i", u=2, e=2, i=d)[
+                        :, :, :, :, i0:i1
+                    ],
                 )
             x_sorted[chunk] = ordered
 
         def transpose(chunk):
             l = ORDER[chunk // PASSES]
-            d = IR_DIMS[l]
+            d = IR_DIMS[l] if IR_DIMS[l] > 1 else PASSES
             as_words = x_sorted[chunk][:].bitcast(F32)
             x_grouped[chunk] = []
             for i0 in range(0, d, 2):
@@ -148,14 +158,16 @@ def tile_so3_linear_pa_kernel(
             l, g = ORDER[chunk // PASSES], chunk % PASSES
             d = IR_DIMS[l]
             if g == 0:
-                codes = keep.tile([P, PASSES, d, P], U32, name="x_codes%d" % l, align_bytes=64)
-                scales = keep.tile([P, PASSES, d, P], U8, name="x_scales%d" % l, align_bytes=64)
+                codes = keep.tile([P, PASSES * d, P], U32, name="x_codes%d" % l, align_bytes=64)
+                scales = keep.tile([P, PASSES * d, P], U8, name="x_scales%d" % l, align_bytes=64)
                 x_codes[l], x_scales[l] = codes, scales
-            for i0 in range(0, d, 2):
-                count = min(2, d - i0)
+            planes = d if d > 1 else PASSES
+            for i0 in range(0, planes, 2):
+                count = min(2, planes - i0)
+                first = g * d + i0
                 nc.vector.quantize_mx(
-                    out=x_codes[l][:, g, i0 : i0 + count, :].rearrange("p c b -> p (c b)").bitcast(FP8X4),
-                    scales=x_scales[l][:, g, i0 : i0 + count, :].rearrange("p c b -> p (c b)"),
+                    out=x_codes[l][:, first : first + count, :].rearrange("p c b -> p (c b)").bitcast(FP8X4),
+                    scales=x_scales[l][:, first : first + count, :].rearrange("p c b -> p (c b)"),
                     in_=x_grouped[chunk][i0 // 2][:, : count * P * 4],
                 )
 
@@ -171,9 +183,9 @@ def tile_so3_linear_pa_kernel(
                     y_banks[(step, i)] = bank
                 nc.tensor.matmul_mx(
                     out=y_banks[(step, i)][:],
-                    lhsT=x_codes[l][:, g, i, :].bitcast(FP8X4),
-                    lhsT_scale=x_scales[l][:, g, i, :],
-                    rhs=w_codes[step][:, g, :].bitcast(FP8X4),
+                    lhsT=x_codes[l][:, g * d + i, :].bitcast(FP8X4),
+                    lhsT_scale=x_scales[l][:, g * d + i, :],
+                    rhs=w_codes[(l, r)][:, g, :].bitcast(FP8X4),
                     rhs_scale=w_scales[l][4 * g : P, N_TILE * r : N_TILE * (r + 1)],
                     start=(g == 0),
                     stop=(g == PASSES - 1),
@@ -223,23 +235,24 @@ def tile_so3_linear_pa_kernel(
             first = SEG_START[l] + N_TILE * d * r
             nc.sync.dma_start(out=out[:, first : first + N_TILE * d], in_=results[step][:, : N_TILE * d])
 
-        load_w_scales(ORDER[0], nc.scalar)
+        first_l, second_l, third_l, last_l = ORDER
+        load_w_scales(first_l, nc.scalar)
         for l in ORDER[1:]:
             load_w_scales(l, nc.gpsimd)
-        for chunk in range(PASSES):
-            load_x(chunk)
+        for g in range(PASSES):
+            load_x(first_l, (g,))
         for r in range(N_TILES):
-            load_w_codes(r)
-            load_x(PASSES + r)
-        for r in range(N_TILES):
-            load_w_codes(N_TILES + r)
+            load_w_codes(first_l, (r,), 0)
+            load_x(second_l, (r,))
+        load_w_codes(second_l, (0,), 1)
+        load_w_codes(second_l, (1, 2), 1)
 
         spread_bias()
         sort(0)
         sort(1)
         sort(2)
-        for chunk in range(2 * PASSES, 3 * PASSES):
-            load_x(chunk)
+        load_x(third_l, (0,))
+        load_x(third_l, (1, 2))
         transpose(0)
         quantise(0)
         transpose(1)
@@ -249,7 +262,7 @@ def tile_so3_linear_pa_kernel(
         sort(3)
 
         for step in range(N_TILES):
-            multiply(step, range(IR_DIMS[ORDER[0]]))
+            multiply(step, range(IR_DIMS[first_l]))
             transpose(step + PASSES)
             if step < N_TILES - 1:
                 interleave(step)
@@ -272,21 +285,19 @@ def tile_so3_linear_pa_kernel(
             else:
                 multiply(step, front)
             if step == N_TILES:
-                for later in range(2 * N_TILES, 3 * N_TILES):
-                    load_w_codes(later)
+                load_w_codes(third_l, range(N_TILES), 2)
             if step > N_TILES:
                 interleave(step - 1)
                 store(step - 1)
             if step == N_TILES + 1:
-                for later in range(3 * N_TILES, STEPS):
-                    load_x(later)
-                load_w_codes(3 * N_TILES)
+                load_x(last_l, range(PASSES))
+                load_w_codes(last_l, (0,), 0)
             if step == N_TILES + 2:
-                load_w_codes(3 * N_TILES + 1)
-                load_w_codes(3 * N_TILES + 2)
-            if step + PASSES + 1 < STEPS:
+                load_w_codes(last_l, (1,), 0)
+                load_w_codes(last_l, (2,), 0)
+            if step + PASSES + 1 <= LAST_CHUNK:
                 sort(step + PASSES + 1)
-            if step + PASSES < STEPS:
+            if step + PASSES <= LAST_CHUNK:
                 transpose(step + PASSES)
                 quantise(step + PASSES)
             multiply(step, range((d + 1) // 2, d))

@@ -94,7 +94,14 @@ def tile_so3_linear_pa_kernel(
                 in_=words_in[l].rearrange("g p n t -> p g (n t)")[:, :, 4 * a : 4 * b].bitcast(I32),
             )
             for r in tiles:
-                w_codes[(l, r)] = codes[:, :, N_TILE * r - a : N_TILE * (r + 1) - a]
+                for g in range(PASSES):
+                    w_codes[(l, g, r)] = codes[:, g, N_TILE * r - a : N_TILE * (r + 1) - a]
+
+        def load_w_pass(l, g, place):
+            codes = keep.tile([P, CHANNELS], U32, name="w_codes", tag="w_codes_%d_%d" % (place, g), align_bytes=64)
+            nc.sync.dma_start(out=codes[:].bitcast(I32), in_=words_in[l][g].rearrange("p n t -> p (n t)").bitcast(I32))
+            for r in range(N_TILES):
+                w_codes[(l, g, r)] = codes[:, N_TILE * r : N_TILE * (r + 1)]
 
         def spread_bias():
             nc.vector.tensor_copy(out=bias_row[0:1, :], in_=bias_in[:])
@@ -185,7 +192,7 @@ def tile_so3_linear_pa_kernel(
                     out=y_banks[(step, i)][:],
                     lhsT=x_codes[l][:, g * d + i, :].bitcast(FP8X4),
                     lhsT_scale=x_scales[l][:, g * d + i, :],
-                    rhs=w_codes[(l, r)][:, g, :].bitcast(FP8X4),
+                    rhs=w_codes[(l, g, r)].bitcast(FP8X4),
                     rhs_scale=w_scales[l][4 * g : P, N_TILE * r : N_TILE * (r + 1)],
                     start=(g == 0),
                     stop=(g == PASSES - 1),
@@ -245,13 +252,13 @@ def tile_so3_linear_pa_kernel(
             load_w_codes(first_l, (r,), 0)
             load_x(second_l, (r,))
         load_w_codes(second_l, (0,), 1)
-        load_w_codes(second_l, (1, 2), 1)
 
         spread_bias()
         sort(0)
         sort(1)
         sort(2)
         load_x(third_l, (0,))
+        load_w_codes(second_l, (1, 2), 1)
         load_x(third_l, (1, 2))
         transpose(0)
         quantise(0)
@@ -265,15 +272,13 @@ def tile_so3_linear_pa_kernel(
             multiply(step, range(IR_DIMS[first_l]))
             transpose(step + PASSES)
             if step < N_TILES - 1:
-                interleave(step)
-                store(step)
                 sort(step + PASSES + 1)
                 quantise(step + PASSES)
             else:
                 quantise(step + PASSES)
-                interleave(step)
-                store(step)
                 sort(step + PASSES + 1)
+            interleave(step)
+            store(step)
 
         for step in range(N_TILES, STEPS):
             d = IR_DIMS[ORDER[step // N_TILES]]
@@ -291,10 +296,10 @@ def tile_so3_linear_pa_kernel(
                 store(step - 1)
             if step == N_TILES + 1:
                 load_x(last_l, range(PASSES))
-                load_w_codes(last_l, (0,), 0)
+                load_w_pass(last_l, 0, 0)
             if step == N_TILES + 2:
-                load_w_codes(last_l, (1,), 0)
-                load_w_codes(last_l, (2,), 0)
+                load_w_pass(last_l, 1, 0)
+                load_w_pass(last_l, 2, 0)
             if step + PASSES + 1 <= LAST_CHUNK:
                 sort(step + PASSES + 1)
             if step + PASSES <= LAST_CHUNK:

@@ -20,6 +20,9 @@ MAX_DIM = 7
 ORDER = (1, 3, 2, 0)
 LAST_CHUNK = 9
 PIECES = {8: 4, 7: 2}
+BORROWED = (7,)
+SHARED = (8,)
+HALVED = 8
 SMALL_DIM = 3
 STEPS = len(ORDER) * PASSES
 OPEN_UNITS = 4
@@ -51,6 +54,7 @@ def tile_so3_linear_pa_kernel(
         y_banks = {}
         y_planes = {}
         results = {}
+        pair = []
 
         bias_in = keep.tile([1, CHANNELS], BF16)
         nc.scalar.dma_start(out=bias_in[:], in_=bias.unsqueeze(0))
@@ -200,23 +204,57 @@ def tile_so3_linear_pa_kernel(
                 if g == PASSES - 1 and d > 1:
                     nc.scalar.copy(out=y_planes[step][:, i, :], in_=y_banks[(step, i)][:])
 
+        def multiply_halves(step):
+            l, r = ORDER[step // N_TILES], step % N_TILES
+            d = IR_DIMS[l]
+            half = N_TILE // 2
+            planes = stage.tile([P, MAX_DIM, N_TILE], F32, name="y_planes")
+            y_planes[step] = planes
+            for h in range(2):
+                for i0 in range(0, d, 2):
+                    count = min(2, d - i0)
+                    bank = psum.tile([P, 2, half], F32, name="bank")
+                    for c in range(count):
+                        for g in range(PASSES):
+                            nc.tensor.matmul_mx(
+                                out=bank[:, c, :],
+                                lhsT=x_codes[l][:, g * d + i0 + c, :].bitcast(FP8X4),
+                                lhsT_scale=x_scales[l][:, g * d + i0 + c, :],
+                                rhs=w_codes[(l, g, r)][:, half * h : half * (h + 1)].bitcast(FP8X4),
+                                rhs_scale=w_scales[l][4 * g : P, N_TILE * r + half * h : N_TILE * r + half * (h + 1)],
+                                start=(g == 0),
+                                stop=(g == PASSES - 1),
+                            )
+                    nc.scalar.copy(out=planes[:, i0 : i0 + count, half * h : half * (h + 1)], in_=bank[:, :count, :])
+                interleave(step, range(h * PIECES[step] // 2, (h + 1) * PIECES[step] // 2))
+
         def multiply(step, components):
             for i in components:
                 passes(step, i, range(PASSES))
 
-        def interleave(step):
+        def interleave(step, some_pieces=None):
             l, r = ORDER[step // N_TILES], step % N_TILES
             d = IR_DIMS[l]
-            if d > SMALL_DIM:
+            if some_pieces is not None and some_pieces[0] > 0:
+                result = results[step]
+            elif step in BORROWED:
+                result = keep.tile([P, N_TILE * d], F32, name="result_borrowed", tag="w_codes_1_1", align_bytes=64)
+            elif d > SMALL_DIM:
                 result = stage.tile([P, N_TILE * MAX_DIM], F32, name="result")
             else:
-                result = stage.tile([P, N_TILE * SMALL_DIM], F32, name="result_small", bufs=N_TILES)
+                if d == 1 and r == 1:
+                    result = pair[0][:, N_TILE:]
+                else:
+                    result = stage.tile([P, N_TILE * SMALL_DIM], F32, name="result_small", bufs=N_TILES)
+                if d == 1 and r == 0:
+                    pair.append(result)
             if d > 1:
                 pieces = PIECES.get(step, 1)
                 width = N_TILE // pieces
                 first = SEG_START[l] + N_TILE * d * r
-                for k in range(pieces):
-                    nc.vector.tensor_copy(
+                for k in some_pieces if some_pieces is not None else range(pieces):
+                    copy_piece = nc.scalar.copy if (step in SHARED and k % 2 == 1) else nc.vector.tensor_copy
+                    copy_piece(
                         out=result[:, width * d * k : width * d * (k + 1)].rearrange("b (m n i) -> b m i n", n=READ_RUN, i=d),
                         in_=y_planes[step][:, :d, width * k : width * (k + 1)].rearrange("b i (m n) -> b m i n", n=READ_RUN),
                     )
@@ -240,6 +278,11 @@ def tile_so3_linear_pa_kernel(
             if PIECES.get(step, 1) > 1:
                 return
             first = SEG_START[l] + N_TILE * d * r
+            if d == 1 and r == 0:
+                return
+            if d == 1 and r == 1:
+                nc.sync.dma_start(out=out[:, first - N_TILE : first + N_TILE], in_=pair[0][:, : 2 * N_TILE])
+                return
             nc.sync.dma_start(out=out[:, first : first + N_TILE * d], in_=results[step][:, : N_TILE * d])
 
         first_l, second_l, third_l, last_l = ORDER
@@ -287,11 +330,11 @@ def tile_so3_linear_pa_kernel(
                 for g in range(PASSES):
                     for i in front:
                         passes(step, i, (g,))
-            else:
+            elif step != HALVED:
                 multiply(step, front)
             if step == N_TILES:
                 load_w_codes(third_l, range(N_TILES), 2)
-            if step > N_TILES:
+            if step > N_TILES and step - 1 != HALVED:
                 interleave(step - 1)
                 store(step - 1)
             if step == N_TILES + 1:
@@ -305,6 +348,9 @@ def tile_so3_linear_pa_kernel(
             if step + PASSES <= LAST_CHUNK:
                 transpose(step + PASSES)
                 quantise(step + PASSES)
-            multiply(step, range((d + 1) // 2, d))
+            if step == HALVED:
+                multiply_halves(step)
+            else:
+                multiply(step, range((d + 1) // 2, d))
         interleave(STEPS - 1)
         store(STEPS - 1)

@@ -23,6 +23,7 @@ PIECES = {8: 4, 7: 2}
 BORROWED = (7,)
 SHARED = (8,)
 HALVED = 8
+WARM_UP = 3
 SMALL_DIM = 3
 STEPS = len(ORDER) * PASSES
 OPEN_UNITS = 4
@@ -308,6 +309,9 @@ def tile_so3_linear_pa_kernel(
         transpose(1)
         quantise(1)
         transpose(2)
+        for k in range(WARM_UP):
+            idle_bank = psum.tile([P, N_TILE], F32, name="bank")
+            nc.tensor.matmul(out=idle_bank[:], lhsT=ones[:], rhs=bias_rows[:, :N_TILE], start=True, stop=True)
         quantise(2)
         sort(3)
 

@@ -23,7 +23,7 @@ PIECES = {8: 4, 7: 2}
 BORROWED = (7,)
 SHARED = (8,)
 HALVED = 8
-WARM_UP = 3
+WARM_UP = 4
 SMALL_DIM = 3
 STEPS = len(ORDER) * PASSES
 OPEN_UNITS = 4
@@ -55,14 +55,13 @@ def tile_so3_linear_pa_kernel(
         y_banks = {}
         y_planes = {}
         results = {}
+        bias_banks = []
         pair = []
 
-        bias_in = keep.tile([1, CHANNELS], BF16)
-        nc.scalar.dma_start(out=bias_in[:], in_=bias.unsqueeze(0))
-        identity = keep.tile([P, P], F32)
-        make_identity(nc, identity[:])
         bias_row = stage.tile([P, CHANNELS], BF16, name="bias_row", tag="y_planes")
         ones = keep.tile([P, P], BF16)
+        zeros = keep.tile([P, N_TILE], BF16)
+        identity = keep.tile([P, P], F32)
         bias_rows = keep.tile([P, CHANNELS], BF16)
 
         for l in ORDER:
@@ -74,7 +73,10 @@ def tile_so3_linear_pa_kernel(
             w_scales[l] = planes
             if l == ORDER[0]:
                 nc.vector.memset(bias_row[:], 0.0)
+                nc.gpsimd.dma_start(out=bias_row[0:1, :], in_=bias.unsqueeze(0))
+                make_identity(nc, identity[:])
                 nc.vector.memset(ones[:], 1.0)
+                nc.vector.memset(zeros[:], 0.0)
 
         def load_x(l, some_passes):
             if l not in x_raw:
@@ -108,17 +110,19 @@ def tile_so3_linear_pa_kernel(
             for r in range(N_TILES):
                 w_codes[(l, g, r)] = codes[:, N_TILE * r : N_TILE * (r + 1)]
 
-        def spread_bias():
-            nc.vector.tensor_copy(out=bias_row[0:1, :], in_=bias_in[:])
+        def spread_bias(r):
+            if r % 2 == 0:
+                bank = psum.tile([P, 2 * N_TILE], BF16, name="bank")
+                bias_banks.append(bank)
+            nc.tensor.matmul(
+                out=bias_banks[r // 2][:, N_TILE * (r % 2) : N_TILE * (r % 2 + 1)], lhsT=ones[:],
+                rhs=bias_row[:, N_TILE * r : N_TILE * (r + 1)], start=True, stop=True,
+            )
+
+        def keep_bias():
             for first in range(0, CHANNELS, 2 * N_TILE):
                 width = min(2 * N_TILE, CHANNELS - first)
-                bank = psum.tile([P, 2 * N_TILE], BF16, name="bank")
-                for n0 in range(0, width, N_TILE):
-                    nc.tensor.matmul(
-                        out=bank[:, n0 : n0 + N_TILE], lhsT=ones[:], rhs=bias_row[:, first + n0 : first + n0 + N_TILE],
-                        start=True, stop=True,
-                    )
-                nc.scalar.copy(out=bias_rows[:, first : first + width], in_=bank[:, :width])
+                nc.scalar.copy(out=bias_rows[:, first : first + width], in_=bias_banks[first // (2 * N_TILE)][:, :width])
 
         def sort(chunk):
             l, g = ORDER[chunk // PASSES], chunk % PASSES
@@ -297,26 +301,28 @@ def tile_so3_linear_pa_kernel(
             load_x(second_l, (r,))
         load_w_codes(second_l, (0,), 1)
 
-        spread_bias()
+        idle_bank = psum.tile([P, N_TILE], F32, name="bank")
+        for k in range(WARM_UP):
+            nc.tensor.matmul(out=idle_bank[:], lhsT=ones[:], rhs=zeros[:], start=True, stop=True)
         sort(0)
         sort(1)
         sort(2)
         load_x(third_l, (0,))
         load_w_codes(second_l, (1, 2), 1)
         load_x(third_l, (1, 2))
-        transpose(0)
-        quantise(0)
-        transpose(1)
-        quantise(1)
-        transpose(2)
-        for k in range(WARM_UP):
-            idle_bank = psum.tile([P, N_TILE], F32, name="bank")
-            nc.tensor.matmul(out=idle_bank[:], lhsT=ones[:], rhs=bias_rows[:, :N_TILE], start=True, stop=True)
-        quantise(2)
+        for chunk in range(PASSES):
+            transpose(chunk)
+            spread_bias(chunk)
+            quantise(chunk)
+        keep_bias()
         sort(3)
 
         for step in range(N_TILES):
-            multiply(step, range(IR_DIMS[first_l]))
+            if step == 0:
+                for i, some_passes in ((0, (0,)), (1, (0,)), (0, (1,)), (1, (1,)), (2, (0, 1)), (0, (2,)), (1, (2,)), (2, (2,))):
+                    passes(step, i, some_passes)
+            else:
+                multiply(step, range(IR_DIMS[first_l]))
             transpose(step + PASSES)
             if step < N_TILES - 1:
                 sort(step + PASSES + 1)

@@ -60,12 +60,12 @@ def tile_so3_linear_pa_kernel(
 
         bias_row = stage.tile([P, CHANNELS], BF16, name="bias_row", tag="y_planes")
         ones = keep.tile([P, P], BF16)
-        zeros = keep.tile([P, N_TILE], BF16)
+        zeros = stage.tile([P, N_TILE], BF16, name="zeros", tag="grouped", bufs=4, align_bytes=64)
         identity = keep.tile([P, P], F32)
         bias_rows = keep.tile([P, CHANNELS], BF16)
 
         for l in ORDER:
-            planes = keep.tile([P, CHANNELS], U8, name="w_scales%d" % l, align_bytes=64)
+            planes = keep.tile([P, CHANNELS], U8, name="w_scales%d" % l, align_bytes=256)
             if l in ORDER[:2]:
                 nc.vector.memset(planes[:].bitcast(I32), 0)
             else:
@@ -95,7 +95,7 @@ def tile_so3_linear_pa_kernel(
 
         def load_w_codes(l, tiles, place):
             a, b = N_TILE * tiles[0], N_TILE * (tiles[-1] + 1)
-            codes = keep.tile([P, PASSES, b - a], U32, name="w_codes", tag="w_codes_%d_%d" % (place, tiles[0]), align_bytes=64)
+            codes = keep.tile([P, PASSES, b - a], U32, name="w_codes", tag="w_codes_%d_%d" % (place, tiles[0]), align_bytes=256)
             nc.sync.dma_start(
                 out=codes[:].bitcast(I32),
                 in_=words_in[l].rearrange("g p n t -> p g (n t)")[:, :, 4 * a : 4 * b].bitcast(I32),
@@ -105,7 +105,7 @@ def tile_so3_linear_pa_kernel(
                     w_codes[(l, g, r)] = codes[:, g, N_TILE * r - a : N_TILE * (r + 1) - a]
 
         def load_w_pass(l, g, place):
-            codes = keep.tile([P, CHANNELS], U32, name="w_codes", tag="w_codes_%d_%d" % (place, g), align_bytes=64)
+            codes = keep.tile([P, CHANNELS], U32, name="w_codes", tag="w_codes_%d_%d" % (place, g), align_bytes=256)
             nc.sync.dma_start(out=codes[:].bitcast(I32), in_=words_in[l][g].rearrange("p n t -> p (n t)").bitcast(I32))
             for r in range(N_TILES):
                 w_codes[(l, g, r)] = codes[:, N_TILE * r : N_TILE * (r + 1)]
@@ -174,8 +174,8 @@ def tile_so3_linear_pa_kernel(
             l, g = ORDER[chunk // PASSES], chunk % PASSES
             d = IR_DIMS[l]
             if g == 0:
-                codes = keep.tile([P, PASSES * d, P], U32, name="x_codes%d" % l, align_bytes=64)
-                scales = keep.tile([P, PASSES * d, P], U8, name="x_scales%d" % l, align_bytes=64)
+                codes = keep.tile([P, PASSES * d, P], U32, name="x_codes%d" % l, align_bytes=256)
+                scales = keep.tile([P, PASSES * d, P], U8, name="x_scales%d" % l, align_bytes=256)
                 x_codes[l], x_scales[l] = codes, scales
             planes = d if d > 1 else PASSES
             for i0 in range(0, planes, 2):
@@ -243,7 +243,7 @@ def tile_so3_linear_pa_kernel(
             if some_pieces is not None and some_pieces[0] > 0:
                 result = results[step]
             elif step in BORROWED:
-                result = keep.tile([P, N_TILE * d], F32, name="result_borrowed", tag="w_codes_1_1", align_bytes=64)
+                result = keep.tile([P, N_TILE * d], F32, name="result_borrowed", tag="w_codes_1_1", align_bytes=256)
             elif d > SMALL_DIM:
                 result = stage.tile([P, N_TILE * MAX_DIM], F32, name="result")
             else:

@@ -59,7 +59,7 @@ def tile_so3_linear_pa_kernel(
         pair = []
 
         bias_row = stage.tile([P, CHANNELS], BF16, name="bias_row", tag="y_planes")
-        ones = keep.tile([P, P], BF16)
+        ones = stage.tile([P, P], BF16, name="ones", tag="y_planes")
         zeros = stage.tile([P, N_TILE], BF16, name="zeros", tag="grouped", bufs=4, align_bytes=64)
         identity = keep.tile([P, P], F32)
         bias_rows = keep.tile([P, CHANNELS], BF16)
@@ -80,7 +80,7 @@ def tile_so3_linear_pa_kernel(
 
         def load_x(l, some_passes):
             if l not in x_raw:
-                raw = keep.tile([P, CHANNELS * IR_DIMS[l]], BF16, name="x_raw", tag="x_raw_%d" % (ORDER.index(l) % 2))
+                raw = keep.tile([P, CHANNELS * IR_DIMS[l]], BF16, name="x_raw", tag="x_raw_%d" % (ORDER.index(l) % 2), align_bytes=256)
                 x_raw[l] = raw
             width = K_PASS * IR_DIMS[l]
             a, b = width * some_passes[0], width * (some_passes[-1] + 1)
@@ -245,12 +245,12 @@ def tile_so3_linear_pa_kernel(
             elif step in BORROWED:
                 result = keep.tile([P, N_TILE * d], F32, name="result_borrowed", tag="w_codes_1_1", align_bytes=256)
             elif d > SMALL_DIM:
-                result = stage.tile([P, N_TILE * MAX_DIM], F32, name="result")
+                result = stage.tile([P, N_TILE * MAX_DIM], F32, name="result", align_bytes=256)
             else:
                 if d == 1 and r == 1:
                     result = pair[0][:, N_TILE:]
                 else:
-                    result = stage.tile([P, N_TILE * SMALL_DIM], F32, name="result_small", bufs=N_TILES)
+                    result = stage.tile([P, N_TILE * SMALL_DIM], F32, name="result_small", bufs=N_TILES, align_bytes=256)
                 if d == 1 and r == 0:
                     pair.append(result)
             if d > 1:

from concourse import mybir
from concourse.masks import make_identity

F32 = mybir.dt.float32
BF16 = mybir.dt.bfloat16
I32 = mybir.dt.int32
U32 = mybir.dt.uint32
U8 = mybir.dt.uint8
FP8X4 = mybir.dt.float8_e4m3fn_x4

P = 128
CHANNELS = 1536
K_PASS = 512
PASSES = CHANNELS // K_PASS
N_TILE = 512
N_TILES = CHANNELS // N_TILE
IR_DIMS = (1, 3, 5, 7)
SEG_START = (0, 1536, 6144, 13824)
MAX_DIM = 7
ORDER = (1, 3, 2, 0)
LAST_CHUNK = 9
PIECES = {8: 4, 7: 2}
BORROWED = (7,)
SHARED = (8,)
HALVED = 8
WARM_UP = 4
SMALL_DIM = 3
STEPS = len(ORDER) * PASSES
OPEN_UNITS = 4
READ_RUN = 2

FLOPS = 2 * P * sum(IR_DIMS) * CHANNELS * CHANNELS


def tile_so3_linear_pa_kernel(
    tc, x, W0_words, W0_scales, W1_words, W1_scales, W2_words, W2_scales, W3_words, W3_scales, bias, out
):
    nc = tc.nc
    words_in = (W0_words, W1_words, W2_words, W3_words)
    scales_in = (W0_scales, W1_scales, W2_scales, W3_scales)

    with (
        tc.tile_pool(name="keep", bufs=1) as keep,
        tc.tile_pool(name="stage", bufs=2) as stage,
        tc.psum_pool(name="psum", bufs=4) as psum,
        tc.manual_schedule(),
    ):
        x_raw = {}
        x_sorted = {}
        x_grouped = {}
        x_codes = {}
        x_scales = {}
        w_codes = {}
        w_scales = {}
        y_banks = {}
        y_planes = {}
        results = {}
        bias_banks = []
        pair = []

        bias_row = stage.tile([P, CHANNELS], BF16, name="bias_row", tag="y_planes")
        ones = stage.tile([P, P], BF16, name="ones", tag="y_planes")
        zeros = stage.tile([P, N_TILE], BF16, name="zeros", tag="grouped", bufs=4, align_bytes=64)
        identity = keep.tile([P, P], F32)
        bias_rows = keep.tile([P, CHANNELS], BF16)

        for l in ORDER:
            planes = keep.tile([P, CHANNELS], U8, name="w_scales%d" % l, align_bytes=256)
            if l in ORDER[:2]:
                nc.vector.memset(planes[:].bitcast(I32), 0)
            else:
                nc.gpsimd.memset(planes[:].bitcast(F32), 0.0)
            w_scales[l] = planes
            if l == ORDER[0]:
                nc.vector.memset(bias_row[:], 0.0)
                nc.gpsimd.dma_start(out=bias_row[0:1, :], in_=bias.unsqueeze(0))
                make_identity(nc, identity[:])
                nc.vector.memset(ones[:], 1.0)
                nc.vector.memset(zeros[:], 0.0)

        def load_x(l, some_passes):
            if l not in x_raw:
                raw = keep.tile([P, CHANNELS * IR_DIMS[l]], BF16, name="x_raw", tag="x_raw_%d" % (ORDER.index(l) % 2), align_bytes=256)
                x_raw[l] = raw
            width = K_PASS * IR_DIMS[l]
            a, b = width * some_passes[0], width * (some_passes[-1] + 1)
            nc.sync.dma_start(out=x_raw[l][:, a:b], in_=x[:, SEG_START[l] + a : SEG_START[l] + b])

        def load_w_scales(l, queue):
            for quadrant in range(4):
                queue.dma_start(
                    out=w_scales[l][32 * quadrant : 32 * quadrant + 4 * PASSES, :].bitcast(F32),
                    in_=scales_in[l][:, 4 * quadrant : 4 * quadrant + 4, :].bitcast(F32),
                )

        def load_w_codes(l, tiles, place):
            a, b = N_TILE * tiles[0], N_TILE * (tiles[-1] + 1)
            codes = keep.tile([P, PASSES, b - a], U32, name="w_codes", tag="w_codes_%d_%d" % (place, tiles[0]), align_bytes=256)
            nc.sync.dma_start(
                out=codes[:].bitcast(I32),
                in_=words_in[l].rearrange("g p n t -> p g (n t)")[:, :, 4 * a : 4 * b].bitcast(I32),
            )
            for r in tiles:
                for g in range(PASSES):
                    w_codes[(l, g, r)] = codes[:, g, N_TILE * r - a : N_TILE * (r + 1) - a]

        def load_w_pass(l, g, place):
            codes = keep.tile([P, CHANNELS], U32, name="w_codes", tag="w_codes_%d_%d" % (place, g), align_bytes=256)
            nc.sync.dma_start(out=codes[:].bitcast(I32), in_=words_in[l][g].rearrange("p n t -> p (n t)").bitcast(I32))
            for r in range(N_TILES):
                w_codes[(l, g, r)] = codes[:, N_TILE * r : N_TILE * (r + 1)]

        def spread_bias(r):
            if r % 2 == 0:
                bank = psum.tile([P, 2 * N_TILE], BF16, name="bank")
                bias_banks.append(bank)
            nc.tensor.matmul(
                out=bias_banks[r // 2][:, N_TILE * (r % 2) : N_TILE * (r % 2 + 1)], lhsT=ones[:],
                rhs=bias_row[:, N_TILE * r : N_TILE * (r + 1)], start=True, stop=True,
            )

        def keep_bias():
            for first in range(0, CHANNELS, 2 * N_TILE):
                width = min(2 * N_TILE, CHANNELS - first)
                nc.scalar.copy(out=bias_rows[:, first : first + width], in_=bias_banks[first // (2 * N_TILE)][:, :width])

        def sort(chunk):
            l, g = ORDER[chunk // PASSES], chunk % PASSES
            d = IR_DIMS[l]
            if d == 1:
                ordered = stage.tile([P, K_PASS * MAX_DIM], BF16, name="x_sorted")
                nc.vector.tensor_copy(
                    out=ordered[:, :CHANNELS].rearrange("b (g u p e) -> b g u p e", u=2, e=2, p=P),
                    in_=x_raw[l][:].rearrange("b (g p u e) -> b g u p e", u=2, e=2, p=P),
                )
                x_sorted[chunk] = ordered
                return
            if chunk < PASSES:
                ordered = stage.tile([P, K_PASS * SMALL_DIM], BF16, name="x_sorted_first", bufs=PASSES)
            else:
                ordered = stage.tile([P, K_PASS * MAX_DIM], BF16, name="x_sorted")
            copies = (d + OPEN_UNITS - 1) // OPEN_UNITS
            share = (d + copies - 1) // copies
            for i0 in range(0, d, share):
                i1 = min(i0 + share, d)
                nc.vector.tensor_copy(
                    out=ordered[:, K_PASS * i0 : K_PASS * i1].rearrange("b (i u p e) -> b u p e i", u=2, e=2, p=P),
                    in_=x_raw[l][:, K_PASS * d * g : K_PASS * d * (g + 1)].rearrange("b (p u e i) -> b u p e i", u=2, e=2, i=d)[
                        :, :, :, :, i0:i1
                    ],
                )
            x_sorted[chunk] = ordered

        def transpose(chunk):
            l = ORDER[chunk // PASSES]
            d = IR_DIMS[l] if IR_DIMS[l] > 1 else PASSES
            as_words = x_sorted[chunk][:].bitcast(F32)
            x_grouped[chunk] = []
            for i0 in range(0, d, 2):
                count = min(2, d - i0)
                turned = psum.tile([P, 2, 2, P], F32, name="turned")
                for c in range(count):
                    for u in range(2):
                        first = (2 * (i0 + c) + u) * P
                        nc.tensor.transpose(turned[:, c, u, :], as_words[:, first : first + P], identity[:])
                grouped = stage.tile([P, 2 * P * 4], BF16, name="grouped", bufs=4, align_bytes=64)
                nc.scalar.copy(
                    out=grouped[:].bitcast(F32).rearrange("p (c b u) -> p c b u", c=2, u=2)[:, :count],
                    in_=turned[:, :count].rearrange("p c u b -> p c b u"),
                )
                x_grouped[chunk].append(grouped)

        def quantise(chunk):
            l, g = ORDER[chunk // PASSES], chunk % PASSES
            d = IR_DIMS[l]
            if g == 0:
                codes = keep.tile([P, PASSES * d, P], U32, name="x_codes%d" % l, align_bytes=256)
                scales = keep.tile([P, PASSES * d, P], U8, name="x_scales%d" % l, align_bytes=256)
                x_codes[l], x_scales[l] = codes, scales
            planes = d if d > 1 else PASSES
            for i0 in range(0, planes, 2):
                count = min(2, planes - i0)
                first = g * d + i0
                nc.vector.quantize_mx(
                    out=x_codes[l][:, first : first + count, :].rearrange("p c b -> p (c b)").bitcast(FP8X4),
                    scales=x_scales[l][:, first : first + count, :].rearrange("p c b -> p (c b)"),
                    in_=x_grouped[chunk][i0 // 2][:, : count * P * 4],
                )

        def passes(step, i, some_passes):
            l, r = ORDER[step // N_TILES], step % N_TILES
            d = IR_DIMS[l]
            for g in some_passes:
                if g == 0:
                    if d > 1 and i == 0:
                        planes = stage.tile([P, MAX_DIM, N_TILE], F32, name="y_planes")
                        y_planes[step] = planes
                    bank = psum.tile([P, N_TILE], F32, name="bank")
                    y_banks[(step, i)] = bank
                nc.tensor.matmul_mx(
                    out=y_banks[(step, i)][:],
                    lhsT=x_codes[l][:, g * d + i, :].bitcast(FP8X4),
                    lhsT_scale=x_scales[l][:, g * d + i, :],
                    rhs=w_codes[(l, g, r)].bitcast(FP8X4),
                    rhs_scale=w_scales[l][4 * g : P, N_TILE * r : N_TILE * (r + 1)],
                    start=(g == 0),
                    stop=(g == PASSES - 1),
                )
                if g == PASSES - 1 and d > 1:
                    nc.scalar.copy(out=y_planes[step][:, i, :], in_=y_banks[(step, i)][:])

        def multiply_halves(step):
            l, r = ORDER[step // N_TILES], step % N_TILES
            d = IR_DIMS[l]
            half = N_TILE // 2
            planes = stage.tile([P, MAX_DIM, N_TILE], F32, name="y_planes")
            y_planes[step] = planes
            for h in range(2):
                for i0 in range(0, d, 2):
                    count = min(2, d - i0)
                    bank = psum.tile([P, 2, half], F32, name="bank")
                    for c in range(count):
                        for g in range(PASSES):
                            nc.tensor.matmul_mx(
                                out=bank[:, c, :],
                                lhsT=x_codes[l][:, g * d + i0 + c, :].bitcast(FP8X4),
                                lhsT_scale=x_scales[l][:, g * d + i0 + c, :],
                                rhs=w_codes[(l, g, r)][:, half * h : half * (h + 1)].bitcast(FP8X4),
                                rhs_scale=w_scales[l][4 * g : P, N_TILE * r + half * h : N_TILE * r + half * (h + 1)],
                                start=(g == 0),
                                stop=(g == PASSES - 1),
                            )
                    nc.scalar.copy(out=planes[:, i0 : i0 + count, half * h : half * (h + 1)], in_=bank[:, :count, :])
                interleave(step, range(h * PIECES[step] // 2, (h + 1) * PIECES[step] // 2))

        def multiply(step, components):
            for i in components:
                passes(step, i, range(PASSES))

        def interleave(step, some_pieces=None):
            l, r = ORDER[step // N_TILES], step % N_TILES
            d = IR_DIMS[l]
            if some_pieces is not None and some_pieces[0] > 0:
                result = results[step]
            elif step in BORROWED:
                result = keep.tile([P, N_TILE * d], F32, name="result_borrowed", tag="w_codes_1_1", align_bytes=256)
            elif d > SMALL_DIM:
                result = stage.tile([P, N_TILE * MAX_DIM], F32, name="result", align_bytes=256)
            else:
                if d == 1 and r == 1:
                    result = pair[0][:, N_TILE:]
                else:
                    result = stage.tile([P, N_TILE * SMALL_DIM], F32, name="result_small", bufs=N_TILES, align_bytes=256)
                if d == 1 and r == 0:
                    pair.append(result)
            if d > 1:
                pieces = PIECES.get(step, 1)
                width = N_TILE // pieces
                first = SEG_START[l] + N_TILE * d * r
                for k in some_pieces if some_pieces is not None else range(pieces):
                    copy_piece = nc.scalar.copy if (step in SHARED and k % 2 == 1) else nc.vector.tensor_copy
                    copy_piece(
                        out=result[:, width * d * k : width * d * (k + 1)].rearrange("b (m n i) -> b m i n", n=READ_RUN, i=d),
                        in_=y_planes[step][:, :d, width * k : width * (k + 1)].rearrange("b i (m n) -> b m i n", n=READ_RUN),
                    )
                    if pieces > 1:
                        nc.sync.dma_start(
                            out=out[:, first + width * d * k : first + width * d * (k + 1)],
                            in_=result[:, width * d * k : width * d * (k + 1)],
                        )
            else:
                nc.vector.tensor_tensor(
                    out=result[:, :N_TILE],
                    in0=y_banks[(step, 0)][:],
                    in1=bias_rows[:, N_TILE * r : N_TILE * (r + 1)],
                    op=mybir.AluOpType.add,
                )
            results[step] = result

        def store(step):
            l, r = ORDER[step // N_TILES], step % N_TILES
            d = IR_DIMS[l]
            if PIECES.get(step, 1) > 1:
                return
            first = SEG_START[l] + N_TILE * d * r
            if d == 1 and r == 0:
                return
            if d == 1 and r == 1:
                nc.sync.dma_start(out=out[:, first - N_TILE : first + N_TILE], in_=pair[0][:, : 2 * N_TILE])
                return
            nc.sync.dma_start(out=out[:, first : first + N_TILE * d], in_=results[step][:, : N_TILE * d])

        first_l, second_l, third_l, last_l = ORDER
        load_w_scales(first_l, nc.scalar)
        for l in ORDER[1:]:
            load_w_scales(l, nc.gpsimd)
        for g in range(PASSES):
            load_x(first_l, (g,))
        for r in range(N_TILES):
            load_w_codes(first_l, (r,), 0)
            load_x(second_l, (r,))
        load_w_codes(second_l, (0,), 1)

        idle_bank = psum.tile([P, N_TILE], F32, name="bank")
        for k in range(WARM_UP):
            nc.tensor.matmul(out=idle_bank[:], lhsT=ones[:], rhs=zeros[:], start=True, stop=True)
        sort(0)
        sort(1)
        sort(2)
        load_x(third_l, (0,))
        load_w_codes(second_l, (1, 2), 1)
        load_x(third_l, (1, 2))
        for chunk in range(PASSES):
            transpose(chunk)
            spread_bias(chunk)
            quantise(chunk)
        keep_bias()
        sort(3)

        for step in range(N_TILES):
            if step == 0:
                for i, some_passes in ((0, (0,)), (1, (0,)), (0, (1,)), (1, (1,)), (2, (0, 1)), (0, (2,)), (1, (2,)), (2, (2,))):
                    passes(step, i, some_passes)
            else:
                multiply(step, range(IR_DIMS[first_l]))
            transpose(step + PASSES)
            if step < N_TILES - 1:
                sort(step + PASSES + 1)
                quantise(step + PASSES)
            else:
                quantise(step + PASSES)
                sort(step + PASSES + 1)
            interleave(step)
            store(step)

        for step in range(N_TILES, STEPS):
            d = IR_DIMS[ORDER[step // N_TILES]]
            front = range((d + 1) // 2)
            if step == N_TILES:
                for g in range(PASSES):
                    for i in front:
                        passes(step, i, (g,))
            elif step != HALVED:
                multiply(step, front)
            if step == N_TILES:
                load_w_codes(third_l, range(N_TILES), 2)
            if step > N_TILES and step - 1 != HALVED:
                interleave(step - 1)
                store(step - 1)
            if step == N_TILES + 1:
                load_x(last_l, range(PASSES))
                load_w_pass(last_l, 0, 0)
            if step == N_TILES + 2:
                load_w_pass(last_l, 1, 0)
                load_w_pass(last_l, 2, 0)
            if step + PASSES + 1 <= LAST_CHUNK:
                sort(step + PASSES + 1)
            if step + PASSES <= LAST_CHUNK:
                transpose(step + PASSES)
                quantise(step + PASSES)
            if step == HALVED:
                multiply_halves(step)
            else:
                multiply(step, range((d + 1) // 2, d))
        interleave(STEPS - 1)
        store(STEPS - 1)
